import numpy as np
import ml_dtypes

BF16 = ml_dtypes.bfloat16


def bf(x):
    return np.asarray(x, np.float32).astype(BF16)


def f32(x):
    return np.asarray(x, np.float32)


def f64(x):
    return np.asarray(x).astype(np.float64)


def striped(idx):
    return np.tile(idx.reshape(-1, 16).T, (8, 1))


D, S, H, M, N = 128, 4096, 256, 128, 2048


def setup_inputs():
    return {"table": bf(np.random.standard_normal((D, S))), "w_enc": bf(np.random.standard_normal((D, H)) / np.sqrt(D)), "w_proj": bf(0.3 * np.random.standard_normal((H, M)) / np.sqrt(H)), "offs": striped(np.random.permutation(S)[:N])}


def reference(table, w_enc, w_proj, offs):
    idx = offs[:16].T.reshape(-1)
    h = f64(w_enc).T @ f64(table)[:, idx]
    z = f64(w_proj).T @ h
    return z / np.sqrt(np.sum(z * z, axis=0, keepdims=True))

@@ -1,0 +1,69 @@
+import concourse.mybir as mybir
+
+BF16, F32, U16 = mybir.dt.bfloat16, mybir.dt.float32, mybir.dt.uint16
+ACT = mybir.ActivationFunctionType
+
+P = 128
+S = 4096
+H = 256
+N = 2048
+H_BLOCKS = H // P
+PIECE = 512
+PIECES = N // PIECE
+PIECE_OFFS = PIECE // 16
+
+FLOPS = 2 * P * H * N + 2 * H * P * N + 2 * P * N
+
+
+def tile_momentumcontrast_kernel(tc, table, w_enc, w_proj, offs, out):
+    nc = tc.nc
+    with (
+        tc.tile_pool(name="held", bufs=1) as held,
+        tc.tile_pool(name="work", bufs=2) as work,
+        tc.psum_pool(name="psum", bufs=8) as psum,
+    ):
+        offsets = held.tile([P, N // 16], U16, name="offsets")
+        nc.sync.dma_start(offsets[:], offs)
+        store = held.tile([P, S], BF16, name="store")
+        nc.sync.dma_start(store[:], table)
+        enc = held.tile([P, H], BF16, name="enc")
+        nc.scalar.dma_start(enc[:], w_enc)
+        proj = held.tile([P, H_BLOCKS * P], BF16, name="proj")
+        for b in range(H_BLOCKS):
+            nc.scalar.dma_start(proj[:, b * P : (b + 1) * P], w_proj[b * P : (b + 1) * P, :])
+        ones = held.tile([P, P], BF16, name="ones")
+        nc.vector.memset(ones[:], 1.0)
+
+
+        h_bf = [held.tile([P, H_BLOCKS, PIECE], BF16, name=f"h_bf{p}") for p in range(PIECES)]
+        for p in range(PIECES):
+            picked = store[:].indirect(offsets[:, p * PIECE_OFFS : (p + 1) * PIECE_OFFS])
+            for b in range(H_BLOCKS):
+                h_ps = psum.tile([P, PIECE], F32, name="h_ps", tag="bank")
+                nc.tensor.matmul(h_ps[:], enc[:, b * P : (b + 1) * P], picked, start=True, stop=True)
+                if b == 0:
+                    nc.vector.tensor_copy(h_bf[p][:, b, :], h_ps[:])
+                else:
+                    nc.scalar.activation(h_bf[p][:, b, :], h_ps[:], ACT.Copy)
+
+        for p in range(PIECES):
+            z_ps = psum.tile([P, PIECE], F32, name="z_ps", tag="bank")
+            for b in range(H_BLOCKS):
+                nc.tensor.matmul(
+                    z_ps[:],
+                    proj[:, b * P : (b + 1) * P],
+                    h_bf[p][:, b, :],
+                    start=(b == 0),
+                    stop=(b == H_BLOCKS - 1),
+                )
+
+            z_sq = work.tile([P, PIECE], BF16, name="z_sq")
+            nc.scalar.activation(z_sq[:], z_ps[:], ACT.Square)
+            sum_ps = psum.tile([P, PIECE], F32, name="sum_ps", tag="bank")
+            nc.tensor.matmul(sum_ps[:], ones[:], z_sq[:], start=True, stop=True)
+            inv_len = work.tile([P, PIECE], F32, name="inv_len")
+            nc.scalar.activation(inv_len[:], sum_ps[:], ACT.Abs_reciprocal_sqrt)
+
+            keys = work.tile([P, PIECE], F32, name="keys")
+            nc.vector.tensor_tensor(keys[:], z_ps[:], inv_len[:], mybir.AluOpType.mult)
+            nc.sync.dma_start(out[:, p * PIECE : (p + 1) * PIECE], keys[:])

@@ -11,6 +11,7 @@ H_BLOCKS = H // P
 PIECE = 512
 PIECES = N // PIECE
 PIECE_OFFS = PIECE // 16
+WARM_UPS = 8
 
 FLOPS = 2 * P * H * N + 2 * H * P * N + 2 * P * N
 
@@ -20,6 +21,7 @@ def tile_momentumcontrast_kernel(tc, table, w_enc, w_proj, offs, out):
     with (
         tc.tile_pool(name="held", bufs=1) as held,
         tc.tile_pool(name="work", bufs=2) as work,
+        tc.tile_pool(name="done", bufs=PIECES) as done,
         tc.psum_pool(name="psum", bufs=8) as psum,
     ):
         offsets = held.tile([P, N // 16], U16, name="offsets")
@@ -31,8 +33,12 @@ def tile_momentumcontrast_kernel(tc, table, w_enc, w_proj, offs, out):
         proj = held.tile([P, H_BLOCKS * P], BF16, name="proj")
         for b in range(H_BLOCKS):
             nc.scalar.dma_start(proj[:, b * P : (b + 1) * P], w_proj[b * P : (b + 1) * P, :])
-        ones = held.tile([P, P], BF16, name="ones")
+        ones = held.tile([P, PIECE], BF16, name="ones")
         nc.vector.memset(ones[:], 1.0)
+
+        warm_ps = psum.tile([P, PIECE], F32, name="warm_ps", tag="bank")
+        for w in range(WARM_UPS):
+            nc.tensor.matmul(warm_ps[:], ones[:, 0:P], ones[:], start=True, stop=True)
 
 
         h_bf = [held.tile([P, H_BLOCKS, PIECE], BF16, name=f"h_bf{p}") for p in range(PIECES)]
@@ -41,29 +47,35 @@ def tile_momentumcontrast_kernel(tc, table, w_enc, w_proj, offs, out):
             for b in range(H_BLOCKS):
                 h_ps = psum.tile([P, PIECE], F32, name="h_ps", tag="bank")
                 nc.tensor.matmul(h_ps[:], enc[:, b * P : (b + 1) * P], picked, start=True, stop=True)
-                if b == 0:
-                    nc.vector.tensor_copy(h_bf[p][:, b, :], h_ps[:])
-                else:
-                    nc.scalar.activation(h_bf[p][:, b, :], h_ps[:], ACT.Copy)
+                nc.vector.tensor_copy(h_bf[p][:, b, :], h_ps[:])
 
-        for p in range(PIECES):
-            z_ps = psum.tile([P, PIECE], F32, name="z_ps", tag="bank")
+        z_ps = [None] * PIECES
+        z_sq = [None] * PIECES
+
+        def project(p):
+            z_ps[p] = psum.tile([P, PIECE], F32, name="z_ps", tag="bank")
             for b in range(H_BLOCKS):
                 nc.tensor.matmul(
-                    z_ps[:],
+                    z_ps[p][:],
                     proj[:, b * P : (b + 1) * P],
                     h_bf[p][:, b, :],
                     start=(b == 0),
                     stop=(b == H_BLOCKS - 1),
                 )
+            z_sq[p] = work.tile([P, PIECE], BF16, name="z_sq")
+            nc.scalar.activation(z_sq[p][:], z_ps[p][:], ACT.Square)
 
-            z_sq = work.tile([P, PIECE], BF16, name="z_sq")
-            nc.scalar.activation(z_sq[:], z_ps[:], ACT.Square)
+        def scale(p):
             sum_ps = psum.tile([P, PIECE], F32, name="sum_ps", tag="bank")
-            nc.tensor.matmul(sum_ps[:], ones[:], z_sq[:], start=True, stop=True)
+            nc.tensor.matmul(sum_ps[:], ones[:, 0:P], z_sq[p][:], start=True, stop=True)
             inv_len = work.tile([P, PIECE], F32, name="inv_len")
             nc.scalar.activation(inv_len[:], sum_ps[:], ACT.Abs_reciprocal_sqrt)
-
-            keys = work.tile([P, PIECE], F32, name="keys")
-            nc.vector.tensor_tensor(keys[:], z_ps[:], inv_len[:], mybir.AluOpType.mult)
+            keys = done.tile([P, PIECE], F32, name="keys")
+            nc.vector.tensor_tensor(keys[:], z_ps[p][:], inv_len[:], mybir.AluOpType.mult)
             nc.sync.dma_start(out[:, p * PIECE : (p + 1) * PIECE], keys[:])
+
+        project(0)
+        for p in range(1, PIECES):
+            project(p)
+            scale(p - 1)
+        scale(PIECES - 1)

@@ -62,20 +62,24 @@ def tile_momentumcontrast_kernel(tc, table, w_enc, w_proj, offs, out):
                     start=(b == 0),
                     stop=(b == H_BLOCKS - 1),
                 )
-            z_sq[p] = work.tile([P, PIECE], BF16, name="z_sq")
-            nc.scalar.activation(z_sq[p][:], z_ps[p][:], ACT.Square)
+            z_sq[p] = done.tile([P, PIECE], BF16, name="z_sq")
+            if p % 2 == 0:
+                nc.scalar.activation(z_sq[p][:], z_ps[p][:], ACT.Square)
+            else:
+                z_sb = work.tile([P, PIECE], F32, name="z_sb")
+                nc.vector.tensor_copy(z_sb[:], z_ps[p][:])
+                nc.vector.tensor_tensor(z_sq[p][:], z_ps[p][:], z_sb[:], mybir.AluOpType.mult)
 
         def scale(p):
             sum_ps = psum.tile([P, PIECE], F32, name="sum_ps", tag="bank")
             nc.tensor.matmul(sum_ps[:], ones[:, 0:P], z_sq[p][:], start=True, stop=True)
-            inv_len = work.tile([P, PIECE], F32, name="inv_len")
+            inv_len = done.tile([P, PIECE], F32, name="inv_len")
             nc.scalar.activation(inv_len[:], sum_ps[:], ACT.Abs_reciprocal_sqrt)
             keys = done.tile([P, PIECE], F32, name="keys")
             nc.vector.tensor_tensor(keys[:], z_ps[p][:], inv_len[:], mybir.AluOpType.mult)
             nc.sync.dma_start(out[:, p * PIECE : (p + 1) * PIECE], keys[:])
 
-        project(0)
-        for p in range(1, PIECES):
+        for p in range(PIECES):
             project(p)
-            scale(p - 1)
-        scale(PIECES - 1)
+        for p in range(PIECES):
+            scale(p)

@@ -11,7 +11,6 @@ H_BLOCKS = H // P
 PIECE = 512
 PIECES = N // PIECE
 PIECE_OFFS = PIECE // 16
-WARM_UPS = 8
 
 FLOPS = 2 * P * H * N + 2 * H * P * N + 2 * P * N
 
@@ -33,12 +32,8 @@ def tile_momentumcontrast_kernel(tc, table, w_enc, w_proj, offs, out):
         proj = held.tile([P, H_BLOCKS * P], BF16, name="proj")
         for b in range(H_BLOCKS):
             nc.scalar.dma_start(proj[:, b * P : (b + 1) * P], w_proj[b * P : (b + 1) * P, :])
-        ones = held.tile([P, PIECE], BF16, name="ones")
+        ones = held.tile([P, P], BF16, name="ones")
         nc.vector.memset(ones[:], 1.0)
-
-        warm_ps = psum.tile([P, PIECE], F32, name="warm_ps", tag="bank")
-        for w in range(WARM_UPS):
-            nc.tensor.matmul(warm_ps[:], ones[:, 0:P], ones[:], start=True, stop=True)
 
 
         h_bf = [held.tile([P, H_BLOCKS, PIECE], BF16, name=f"h_bf{p}") for p in range(PIECES)]
@@ -72,7 +67,7 @@ def tile_momentumcontrast_kernel(tc, table, w_enc, w_proj, offs, out):
 
         def scale(p):
             sum_ps = psum.tile([P, PIECE], F32, name="sum_ps", tag="bank")
-            nc.tensor.matmul(sum_ps[:], ones[:, 0:P], z_sq[p][:], start=True, stop=True)
+            nc.tensor.matmul(sum_ps[:], ones[:], z_sq[p][:], start=True, stop=True)
             inv_len = done.tile([P, PIECE], F32, name="inv_len")
             nc.scalar.activation(inv_len[:], sum_ps[:], ACT.Abs_reciprocal_sqrt)
             keys = done.tile([P, PIECE], F32, name="keys")

@@ -42,7 +42,10 @@ def tile_momentumcontrast_kernel(tc, table, w_enc, w_proj, offs, out):
             for b in range(H_BLOCKS):
                 h_ps = psum.tile([P, PIECE], F32, name="h_ps", tag="bank")
                 nc.tensor.matmul(h_ps[:], enc[:, b * P : (b + 1) * P], picked, start=True, stop=True)
-                nc.vector.tensor_copy(h_bf[p][:, b, :], h_ps[:])
+                if b == 0:
+                    nc.scalar.activation(h_bf[p][:, b, :], h_ps[:], ACT.Copy)
+                else:
+                    nc.vector.tensor_copy(h_bf[p][:, b, :], h_ps[:])
 
         z_ps = [None] * PIECES
         z_sq = [None] * PIECES

@@ -35,6 +35,11 @@ def tile_momentumcontrast_kernel(tc, table, w_enc, w_proj, offs, out):
         ones = held.tile([P, P], BF16, name="ones")
         nc.vector.memset(ones[:], 1.0)
 
+        one = held.tile([P, 1], F32, name="one")
+        nc.vector.memset(one[:], 1.0)
+        early = held.tile([P, 1], F32, name="early")
+        nc.scalar.activation(early[:], one[:], ACT.Abs_reciprocal_sqrt)
+
 
         h_bf = [held.tile([P, H_BLOCKS, PIECE], BF16, name=f"h_bf{p}") for p in range(PIECES)]
         for p in range(PIECES):

@@ -66,7 +66,7 @@ def tile_momentumcontrast_kernel(tc, table, w_enc, w_proj, offs, out):
                     stop=(b == H_BLOCKS - 1),
                 )
             z_sq[p] = done.tile([P, PIECE], BF16, name="z_sq")
-            if p % 2 == 0:
+            if p != 2:
                 nc.scalar.activation(z_sq[p][:], z_ps[p][:], ACT.Square)
             else:
                 z_sb = work.tile([P, PIECE], F32, name="z_sb")
@@ -82,7 +82,11 @@ def tile_momentumcontrast_kernel(tc, table, w_enc, w_proj, offs, out):
             nc.vector.tensor_tensor(keys[:], z_ps[p][:], inv_len[:], mybir.AluOpType.mult)
             nc.sync.dma_start(out[:, p * PIECE : (p + 1) * PIECE], keys[:])
 
-        for p in range(PIECES):
-            project(p)
-        for p in range(PIECES):
-            scale(p)
+        project(0)
+        project(1)
+        project(2)
+        scale(0)
+        project(3)
+        scale(1)
+        scale(2)
+        scale(3)

@@ -10,6 +10,7 @@ N = 2048
 H_BLOCKS = H // P
 PIECE = 512
 PIECES = N // PIECE
+HALF = PIECE // 2
 PIECE_OFFS = PIECE // 16
 
 FLOPS = 2 * P * H * N + 2 * H * P * N + 2 * P * N
@@ -77,10 +78,12 @@ def tile_momentumcontrast_kernel(tc, table, w_enc, w_proj, offs, out):
             sum_ps = psum.tile([P, PIECE], F32, name="sum_ps", tag="bank")
             nc.tensor.matmul(sum_ps[:], ones[:], z_sq[p][:], start=True, stop=True)
             inv_len = done.tile([P, PIECE], F32, name="inv_len")
-            nc.scalar.activation(inv_len[:], sum_ps[:], ACT.Abs_reciprocal_sqrt)
             keys = done.tile([P, PIECE], F32, name="keys")
-            nc.vector.tensor_tensor(keys[:], z_ps[p][:], inv_len[:], mybir.AluOpType.mult)
-            nc.sync.dma_start(out[:, p * PIECE : (p + 1) * PIECE], keys[:])
+            for first in range(0, PIECE, HALF):
+                half = slice(first, first + HALF)
+                nc.scalar.activation(inv_len[:, half], sum_ps[:, half], ACT.Abs_reciprocal_sqrt)
+                nc.vector.tensor_tensor(keys[:, half], z_ps[p][:, half], inv_len[:, half], mybir.AluOpType.mult)
+                nc.sync.dma_start(out[:, p * PIECE + first : p * PIECE + first + HALF], keys[:, half])
 
         project(0)
         project(1)

@@ -27,7 +27,8 @@ def tile_momentumcontrast_kernel(tc, table, w_enc, w_proj, offs, out):
         offsets = held.tile([P, N // 16], U16, name="offsets")
         nc.sync.dma_start(offsets[:], offs)
         store = held.tile([P, S], BF16, name="store")
-        nc.sync.dma_start(store[:], table)
+        nc.sync.dma_start(store[:, : S // 2], table[:, : S // 2])
+        nc.scalar.dma_start(store[:, S // 2 :], table[:, S // 2 :])
         enc = held.tile([P, H], BF16, name="enc")
         nc.scalar.dma_start(enc[:], w_enc)
         proj = held.tile([P, H_BLOCKS * P], BF16, name="proj")

@@ -31,9 +31,8 @@ def tile_momentumcontrast_kernel(tc, table, w_enc, w_proj, offs, out):
         nc.scalar.dma_start(store[:, S // 2 :], table[:, S // 2 :])
         enc = held.tile([P, H], BF16, name="enc")
         nc.scalar.dma_start(enc[:], w_enc)
-        proj = held.tile([P, H_BLOCKS * P], BF16, name="proj")
-        for b in range(H_BLOCKS):
-            nc.scalar.dma_start(proj[:, b * P : (b + 1) * P], w_proj[b * P : (b + 1) * P, :])
+        proj = held.tile([P, H_BLOCKS, P], BF16, name="proj")
+        nc.scalar.dma_start(proj[:], w_proj.rearrange("(b p) m -> p b m", p=P))
         ones = held.tile([P, P], BF16, name="ones")
         nc.vector.memset(ones[:], 1.0)
 
@@ -62,7 +61,7 @@ def tile_momentumcontrast_kernel(tc, table, w_enc, w_proj, offs, out):
             for b in range(H_BLOCKS):
                 nc.tensor.matmul(
                     z_ps[p][:],
-                    proj[:, b * P : (b + 1) * P],
+                    proj[:, b, :],
                     h_bf[p][:, b, :],
                     start=(b == 0),
                     stop=(b == H_BLOCKS - 1),

@@ -8,10 +8,11 @@ S = 4096
 H = 256
 N = 2048
 H_BLOCKS = H // P
-PIECE = 512
+BANK = 512
+PIECE = BANK // H_BLOCKS
 PIECES = N // PIECE
-HALF = PIECE // 2
 PIECE_OFFS = PIECE // 16
+LAG = 3
 
 FLOPS = 2 * P * H * N + 2 * H * P * N + 2 * P * N
 
@@ -45,51 +46,43 @@ def tile_momentumcontrast_kernel(tc, table, w_enc, w_proj, offs, out):
         h_bf = [held.tile([P, H_BLOCKS, PIECE], BF16, name=f"h_bf{p}") for p in range(PIECES)]
         for p in range(PIECES):
             picked = store[:].indirect(offsets[:, p * PIECE_OFFS : (p + 1) * PIECE_OFFS])
+            h_ps = psum.tile([P, H_BLOCKS, PIECE], F32, name="h_ps", tag="bank")
             for b in range(H_BLOCKS):
-                h_ps = psum.tile([P, PIECE], F32, name="h_ps", tag="bank")
-                nc.tensor.matmul(h_ps[:], enc[:, b * P : (b + 1) * P], picked, start=True, stop=True)
-                if b == 0:
-                    nc.scalar.activation(h_bf[p][:, b, :], h_ps[:], ACT.Copy)
-                else:
-                    nc.vector.tensor_copy(h_bf[p][:, b, :], h_ps[:])
+                nc.tensor.matmul(h_ps[:, b, :], enc[:, b * P : (b + 1) * P], picked, start=True, stop=True)
+            if p % 2 == 0:
+                nc.scalar.activation(h_bf[p][:], h_ps[:], ACT.Copy)
+            else:
+                nc.vector.tensor_copy(h_bf[p][:], h_ps[:])
 
         z_ps = [None] * PIECES
+        sum_ps = [None] * PIECES
         z_sq = [None] * PIECES
 
         def project(p):
-            z_ps[p] = psum.tile([P, PIECE], F32, name="z_ps", tag="bank")
+            bank = psum.tile([P, 2, PIECE], F32, name="z_and_sum", tag="bank")
+            z_ps[p], sum_ps[p] = bank[:, 0, :], bank[:, 1, :]
             for b in range(H_BLOCKS):
                 nc.tensor.matmul(
-                    z_ps[p][:],
-                    proj[:, b, :],
-                    h_bf[p][:, b, :],
-                    start=(b == 0),
-                    stop=(b == H_BLOCKS - 1),
+                    z_ps[p], proj[:, b, :], h_bf[p][:, b, :], start=(b == 0), stop=(b == H_BLOCKS - 1)
                 )
             z_sq[p] = done.tile([P, PIECE], BF16, name="z_sq")
-            if p != 2:
-                nc.scalar.activation(z_sq[p][:], z_ps[p][:], ACT.Square)
+            if p % 4 != 3:
+                nc.scalar.activation(z_sq[p][:], z_ps[p], ACT.Square)
             else:
                 z_sb = work.tile([P, PIECE], F32, name="z_sb")
-                nc.vector.tensor_copy(z_sb[:], z_ps[p][:])
-                nc.vector.tensor_tensor(z_sq[p][:], z_ps[p][:], z_sb[:], mybir.AluOpType.mult)
+                nc.vector.tensor_copy(z_sb[:], z_ps[p])
+                nc.vector.tensor_tensor(z_sq[p][:], z_ps[p], z_sb[:], mybir.AluOpType.mult)
 
         def scale(p):
-            sum_ps = psum.tile([P, PIECE], F32, name="sum_ps", tag="bank")
-            nc.tensor.matmul(sum_ps[:], ones[:], z_sq[p][:], start=True, stop=True)
+            nc.tensor.matmul(sum_ps[p], ones[:], z_sq[p][:], start=True, stop=True)
             inv_len = done.tile([P, PIECE], F32, name="inv_len")
+            nc.scalar.activation(inv_len[:], sum_ps[p], ACT.Abs_reciprocal_sqrt)
             keys = done.tile([P, PIECE], F32, name="keys")
-            for first in range(0, PIECE, HALF):
-                half = slice(first, first + HALF)
-                nc.scalar.activation(inv_len[:, half], sum_ps[:, half], ACT.Abs_reciprocal_sqrt)
-                nc.vector.tensor_tensor(keys[:, half], z_ps[p][:, half], inv_len[:, half], mybir.AluOpType.mult)
-                nc.sync.dma_start(out[:, p * PIECE + first : p * PIECE + first + HALF], keys[:, half])
+            nc.vector.tensor_tensor(keys[:], z_ps[p], inv_len[:], mybir.AluOpType.mult)
+            nc.sync.dma_start(out[:, p * PIECE : (p + 1) * PIECE], keys[:])
 
-        project(0)
-        project(1)
-        project(2)
-        scale(0)
-        project(3)
-        scale(1)
-        scale(2)
-        scale(3)
+        for step in range(PIECES + LAG):
+            if step < PIECES:
+                project(step)
+            if step >= LAG:
+                scale(step - LAG)

@@ -12,6 +12,7 @@ BANK = 512
 PIECE = BANK // H_BLOCKS
 PIECES = N // PIECE
 PIECE_OFFS = PIECE // 16
+VECTOR_SQUARES = (3, 5)
 LAG = 3
 
 FLOPS = 2 * P * H * N + 2 * H * P * N + 2 * P * N
@@ -66,7 +67,7 @@ def tile_momentumcontrast_kernel(tc, table, w_enc, w_proj, offs, out):
                     z_ps[p], proj[:, b, :], h_bf[p][:, b, :], start=(b == 0), stop=(b == H_BLOCKS - 1)
                 )
             z_sq[p] = done.tile([P, PIECE], BF16, name="z_sq")
-            if p % 4 != 3:
+            if p not in VECTOR_SQUARES:
                 nc.scalar.activation(z_sq[p][:], z_ps[p], ACT.Square)
             else:
                 z_sb = work.tile([P, PIECE], F32, name="z_sb")

@@ -8,10 +8,11 @@ S = 4096
 H = 256
 N = 2048
 H_BLOCKS = H // P
-BANK = 512
-PIECE = BANK // H_BLOCKS
+PIECE = 512
 PIECES = N // PIECE
 PIECE_OFFS = PIECE // 16
+CHUNK = PIECE // 2
+CHUNKS = N // CHUNK
 VECTOR_SQUARES = (3, 5)
 LAG = 3
 
@@ -23,7 +24,7 @@ def tile_momentumcontrast_kernel(tc, table, w_enc, w_proj, offs, out):
     with (
         tc.tile_pool(name="held", bufs=1) as held,
         tc.tile_pool(name="work", bufs=2) as work,
-        tc.tile_pool(name="done", bufs=PIECES) as done,
+        tc.tile_pool(name="done", bufs=CHUNKS) as done,
         tc.psum_pool(name="psum", bufs=8) as psum,
     ):
         offsets = held.tile([P, N // 16], U16, name="offsets")
@@ -47,43 +48,48 @@ def tile_momentumcontrast_kernel(tc, table, w_enc, w_proj, offs, out):
         h_bf = [held.tile([P, H_BLOCKS, PIECE], BF16, name=f"h_bf{p}") for p in range(PIECES)]
         for p in range(PIECES):
             picked = store[:].indirect(offsets[:, p * PIECE_OFFS : (p + 1) * PIECE_OFFS])
-            h_ps = psum.tile([P, H_BLOCKS, PIECE], F32, name="h_ps", tag="bank")
             for b in range(H_BLOCKS):
-                nc.tensor.matmul(h_ps[:, b, :], enc[:, b * P : (b + 1) * P], picked, start=True, stop=True)
-            if p % 2 == 0:
-                nc.scalar.activation(h_bf[p][:], h_ps[:], ACT.Copy)
-            else:
-                nc.vector.tensor_copy(h_bf[p][:], h_ps[:])
+                h_ps = psum.tile([P, PIECE], F32, name="h_ps", tag="bank")
+                nc.tensor.matmul(h_ps[:], enc[:, b * P : (b + 1) * P], picked, start=True, stop=True)
+                if b == 0:
+                    nc.scalar.activation(h_bf[p][:, b, :], h_ps[:], ACT.Copy)
+                else:
+                    nc.vector.tensor_copy(h_bf[p][:, b, :], h_ps[:])
 
-        z_ps = [None] * PIECES
-        sum_ps = [None] * PIECES
-        z_sq = [None] * PIECES
+        z_ps = [None] * CHUNKS
+        sum_ps = [None] * CHUNKS
+        z_sq = [None] * CHUNKS
 
-        def project(p):
-            bank = psum.tile([P, 2, PIECE], F32, name="z_and_sum", tag="bank")
-            z_ps[p], sum_ps[p] = bank[:, 0, :], bank[:, 1, :]
+        def project(c):
+            bank = psum.tile([P, 2, CHUNK], F32, name="z_and_sum", tag="bank")
+            z_ps[c], sum_ps[c] = bank[:, 0, :], bank[:, 1, :]
+            p, first = divmod(c * CHUNK, PIECE)
             for b in range(H_BLOCKS):
                 nc.tensor.matmul(
-                    z_ps[p], proj[:, b, :], h_bf[p][:, b, :], start=(b == 0), stop=(b == H_BLOCKS - 1)
+                    z_ps[c],
+                    proj[:, b, :],
+                    h_bf[p][:, b, first : first + CHUNK],
+                    start=(b == 0),
+                    stop=(b == H_BLOCKS - 1),
                 )
-            z_sq[p] = done.tile([P, PIECE], BF16, name="z_sq")
-            if p not in VECTOR_SQUARES:
-                nc.scalar.activation(z_sq[p][:], z_ps[p], ACT.Square)
+            z_sq[c] = done.tile([P, CHUNK], BF16, name="z_sq")
+            if c not in VECTOR_SQUARES:
+                nc.scalar.activation(z_sq[c][:], z_ps[c], ACT.Square)
             else:
-                z_sb = work.tile([P, PIECE], F32, name="z_sb")
-                nc.vector.tensor_copy(z_sb[:], z_ps[p])
-                nc.vector.tensor_tensor(z_sq[p][:], z_ps[p], z_sb[:], mybir.AluOpType.mult)
+                z_sb = work.tile([P, CHUNK], F32, name="z_sb")
+                nc.vector.tensor_copy(z_sb[:], z_ps[c])
+                nc.vector.tensor_tensor(z_sq[c][:], z_ps[c], z_sb[:], mybir.AluOpType.mult)
 
-        def scale(p):
-            nc.tensor.matmul(sum_ps[p], ones[:], z_sq[p][:], start=True, stop=True)
-            inv_len = done.tile([P, PIECE], F32, name="inv_len")
-            nc.scalar.activation(inv_len[:], sum_ps[p], ACT.Abs_reciprocal_sqrt)
-            keys = done.tile([P, PIECE], F32, name="keys")
-            nc.vector.tensor_tensor(keys[:], z_ps[p], inv_len[:], mybir.AluOpType.mult)
-            nc.sync.dma_start(out[:, p * PIECE : (p + 1) * PIECE], keys[:])
+        def scale(c):
+            nc.tensor.matmul(sum_ps[c], ones[:], z_sq[c][:], start=True, stop=True)
+            inv_len = done.tile([P, CHUNK], F32, name="inv_len")
+            nc.scalar.activation(inv_len[:], sum_ps[c], ACT.Abs_reciprocal_sqrt)
+            keys = done.tile([P, CHUNK], F32, name="keys")
+            nc.vector.tensor_tensor(keys[:], z_ps[c], inv_len[:], mybir.AluOpType.mult)
+            nc.sync.dma_start(out[:, c * CHUNK : (c + 1) * CHUNK], keys[:])
 
-        for step in range(PIECES + LAG):
-            if step < PIECES:
+        for step in range(CHUNKS + LAG):
+            if step < CHUNKS:
                 project(step)
             if step >= LAG:
                 scale(step - LAG)

import concourse.mybir as mybir

BF16, F32, U16 = mybir.dt.bfloat16, mybir.dt.float32, mybir.dt.uint16
ACT = mybir.ActivationFunctionType

P = 128
S = 4096
H = 256
N = 2048
H_BLOCKS = H // P
PIECE = 512
PIECES = N // PIECE
PIECE_OFFS = PIECE // 16
CHUNK = PIECE // 2
CHUNKS = N // CHUNK
VECTOR_SQUARES = (3, 5)
LAG = 3

FLOPS = 2 * P * H * N + 2 * H * P * N + 2 * P * N


def tile_momentumcontrast_kernel(tc, table, w_enc, w_proj, offs, out):
    nc = tc.nc
    with (
        tc.tile_pool(name="held", bufs=1) as held,
        tc.tile_pool(name="work", bufs=2) as work,
        tc.tile_pool(name="done", bufs=CHUNKS) as done,
        tc.psum_pool(name="psum", bufs=8) as psum,
    ):
        offsets = held.tile([P, N // 16], U16, name="offsets")
        nc.sync.dma_start(offsets[:], offs)
        store = held.tile([P, S], BF16, name="store")
        nc.sync.dma_start(store[:, : S // 2], table[:, : S // 2])
        nc.scalar.dma_start(store[:, S // 2 :], table[:, S // 2 :])
        enc = held.tile([P, H], BF16, name="enc")
        nc.scalar.dma_start(enc[:], w_enc)
        proj = held.tile([P, H_BLOCKS, P], BF16, name="proj")
        nc.scalar.dma_start(proj[:], w_proj.rearrange("(b p) m -> p b m", p=P))
        ones = held.tile([P, P], BF16, name="ones")
        nc.vector.memset(ones[:], 1.0)

        one = held.tile([P, 1], F32, name="one")
        nc.vector.memset(one[:], 1.0)
        early = held.tile([P, 1], F32, name="early")
        nc.scalar.activation(early[:], one[:], ACT.Abs_reciprocal_sqrt)


        h_bf = [held.tile([P, H_BLOCKS, PIECE], BF16, name=f"h_bf{p}") for p in range(PIECES)]
        for p in range(PIECES):
            picked = store[:].indirect(offsets[:, p * PIECE_OFFS : (p + 1) * PIECE_OFFS])
            for b in range(H_BLOCKS):
                h_ps = psum.tile([P, PIECE], F32, name="h_ps", tag="bank")
                nc.tensor.matmul(h_ps[:], enc[:, b * P : (b + 1) * P], picked, start=True, stop=True)
                if b == 0:
                    nc.scalar.activation(h_bf[p][:, b, :], h_ps[:], ACT.Copy)
                else:
                    nc.vector.tensor_copy(h_bf[p][:, b, :], h_ps[:])

        z_ps = [None] * CHUNKS
        sum_ps = [None] * CHUNKS
        z_sq = [None] * CHUNKS

        def project(c):
            bank = psum.tile([P, 2, CHUNK], F32, name="z_and_sum", tag="bank")
            z_ps[c], sum_ps[c] = bank[:, 0, :], bank[:, 1, :]
            p, first = divmod(c * CHUNK, PIECE)
            for b in range(H_BLOCKS):
                nc.tensor.matmul(
                    z_ps[c],
                    proj[:, b, :],
                    h_bf[p][:, b, first : first + CHUNK],
                    start=(b == 0),
                    stop=(b == H_BLOCKS - 1),
                )
            z_sq[c] = done.tile([P, CHUNK], BF16, name="z_sq")
            if c not in VECTOR_SQUARES:
                nc.scalar.activation(z_sq[c][:], z_ps[c], ACT.Square)
            else:
                z_sb = work.tile([P, CHUNK], F32, name="z_sb")
                nc.vector.tensor_copy(z_sb[:], z_ps[c])
                nc.vector.tensor_tensor(z_sq[c][:], z_ps[c], z_sb[:], mybir.AluOpType.mult)

        def scale(c):
            nc.tensor.matmul(sum_ps[c], ones[:], z_sq[c][:], start=True, stop=True)
            inv_len = done.tile([P, CHUNK], F32, name="inv_len")
            nc.scalar.activation(inv_len[:], sum_ps[c], ACT.Abs_reciprocal_sqrt)
            keys = done.tile([P, CHUNK], F32, name="keys")
            nc.vector.tensor_tensor(keys[:], z_ps[c], inv_len[:], mybir.AluOpType.mult)
            nc.sync.dma_start(out[:, c * CHUNK : (c + 1) * CHUNK], keys[:])

        for step in range(CHUNKS + LAG):
            if step < CHUNKS:
                project(step)
            if step >= LAG:
                scale(step - LAG)
